import numpy as np
import ml_dtypes


def mxq(x, axis, fmt="e4m3"):
    dtype, down = {"e4m3": (ml_dtypes.float8_e4m3fn, 7), "e5m2": (ml_dtypes.float8_e5m2, 14)}[fmt]
    v = np.moveaxis(np.asarray(x, np.float32).astype(ml_dtypes.bfloat16).astype(np.float64), axis, -1)
    blocks = v.reshape(v.shape[:-1] + (-1, 32))
    amax = np.abs(blocks).max(-1, keepdims=True)
    byte = np.maximum(np.where(amax > 0, np.frexp(amax)[1] - 1 + 127, 0) - down, 1)
    scale = np.exp2(byte - 127.0)
    codes = (blocks / scale).astype(np.float32).astype(dtype).astype(np.float64)
    return np.moveaxis((codes * scale).reshape(v.shape), -1, axis)


WIDE = False


def mx_kscale(k):
    if not WIDE:
        return np.ones(k)
    levels = np.array([10, -10, 5, -5, 0])
    if k % 512:
        return np.exp2(np.random.permutation(np.resize(levels, k // 32))).repeat(32)
    a = np.empty((k // 512, 16))
    for p in range(k // 512):
        a[p, :8] = np.random.permutation(np.resize(levels, 8))
        for g in range(8):
            far = levels[np.abs(levels - a[p, g]) >= 10]
            a[p, g + 8] = far[np.random.randint(len(far))]
    return np.exp2(a.ravel()).repeat(32)


BF16 = ml_dtypes.bfloat16


def bf(x):
    return np.asarray(x, np.float32).astype(BF16)


def f64(x):
    return np.asarray(x).astype(np.float64)


B, S, IN, OUT, A, R = 8, 1024, 1024, 128, 8, 128
G = B // A
SCALING = 2.0


def setup_inputs():
    s = mx_kscale(IN)
    return {"data": bf(np.random.standard_normal((B, S, IN)) * s),
            "W": bf(np.random.standard_normal((OUT, IN)) / np.sqrt(IN) / s),
            "t_lora": bf(np.random.standard_normal((A, G, S, R))),
            "lora_b": bf(np.random.standard_normal((A, OUT, R)) * 0.5 / np.sqrt(R))}


def reference(data, W, t_lora, lora_b):
    base = mxq(f64(data), 2, "e4m3") @ mxq(f64(W), 1, "e4m3").T
    delta = (f64(t_lora).reshape(A, G * S, R) @ f64(lora_b).transpose(0, 2, 1)) * SCALING
    return base + delta.reshape(B, S, OUT)

@@ -1,0 +1,206 @@
+from contextlib import ExitStack
+
+import concourse.mybir as mybir
+from concourse.masks import make_identity
+
+F32 = mybir.dt.float32
+BF16 = mybir.dt.bfloat16
+U32 = mybir.dt.uint32
+U8 = mybir.dt.uint8
+FP8X4 = mybir.dt.float8_e4m3fn_x4
+ADD = mybir.AluOpType.add
+
+P = 128
+A = 8
+S = 1024
+K = 1024
+O = 128
+R = 128
+J = 8
+FLOPS = 2 * A * S * K * O + 2 * A * S * R * O
+
+UNITS = [list(range(4 * c, 4 * c + 4)) for c in range(16)]
+GROUPS = [[u] for u in range(16)]
+STORES = dict([(u, [u]) for u in range(16)])
+LATE_ADAPTER = 7
+V_BANKS = frozenset(range(3, 64, 8))
+
+
+def words_of(q):
+    g, u = divmod(q, 2)
+    return slice(256 * g + u, 256 * (g + 1), 2)
+
+
+def tile_linear_pa_t_kernel(tc, data, W, t_lora, lora_b, out):
+    nc = tc.nc
+    with ExitStack() as ctx:
+        ctx.enter_context(tc.manual_schedule())
+        const = ctx.enter_context(tc.tile_pool(name="const", bufs=1))
+        xpool = ctx.enter_context(tc.tile_pool(name="xpool", bufs=5))
+        ttp = ctx.enter_context(tc.tile_pool(name="ttp", bufs=3))
+        gpool = ctx.enter_context(tc.tile_pool(name="gpool", bufs=4))
+        cpool = ctx.enter_context(tc.tile_pool(name="cpool", bufs=4))
+        psum = ctx.enter_context(tc.psum_pool(name="psum", bufs=1))
+
+        data_v = data.rearrange("a (p j) k -> a p j k", j=J)
+        t_v = t_lora.rearrange("a g (p j) r -> p (a g) (j r)", j=J)
+        out_v = out.rearrange("a (p j) o -> a p (j o)", j=J)
+        lb_v = lora_b.rearrange("a (h l) r -> (a h) (l r)", l=8)
+
+        warm = const.tile([P, 512], BF16, name="warm")
+        nc.vector.memset(warm[:].bitcast(mybir.dt.int32), 0)
+        ident_b = const.tile([P, P], BF16, name="ident_b")
+        ident_f = const.tile([P, P], F32, name="ident_f")
+        make_identity(nc, ident_b[:])
+        make_identity(nc, ident_f[:])
+
+        t_src = {}
+
+        def load_t(a0, n):
+            t_sb = const.tile([P, n, J * R], BF16, name="t_sb%d" % a0)
+            nc.sync.dma_start(out=t_sb[:], in_=t_v[:, a0:a0 + n, :])
+            for i in range(n):
+                t_src[a0 + i] = t_sb[:, i, :]
+
+        load_t(0, 1)
+        lb_sb = const.tile([P, 8 * R], BF16, name="lb_sb")
+        nc.sync.dma_start(out=lb_sb[:], in_=lb_v)
+        load_t(1, 1)
+        w_sb = const.tile([P, K], BF16, name="w_sb")
+        nc.sync.dma_start(out=w_sb[:], in_=W)
+        load_t(2, 2)
+        load_t(4, 4)
+        x_words = {}
+        for c in range(2 * A):
+            a, h = divmod(c, 2)
+            x_half = xpool.tile([P, J // 2, K], BF16, name="x_half", bufs=10)
+            nc.sync.dma_start(out=x_half[:], in_=data_v[a, :, h * 4:(h + 1) * 4, :])
+            for j in range(4):
+                x_words[c * 4 + j] = x_half[:].bitcast(F32)[:, j, :]
+
+        o_sb = [const.tile([P, J * O], F32, name="o_sb%d" % a) for a in range(A)]
+
+        def words_out(on_vector, dst_f32, bank):
+            src = bank[:].rearrange("p (g u) t -> p g t u", u=2)
+            dst = dst_f32.rearrange("p (g t u) -> p g t u", g=2, u=2)
+            if on_vector:
+                nc.vector.tensor_copy(out=dst, in_=src)
+            else:
+                nc.scalar.copy(out=dst, in_=src)
+
+        lbT = const.tile([P, A, O], BF16, name="lbT")
+        w_grp = const.tile([P, K], BF16, name="w_grp", align_bytes=64)
+        w_codes = const.tile([P, K // 4], U32, name="w_codes", align_bytes=64)
+        w_scales = const.tile([P, K // 4], U8, name="w_scales", align_bytes=64)
+        tT = {}
+
+        def lora_transposes(a):
+            tlp = psum.tile([P, J, P], BF16, name="tlp", tag="acc", bufs=2)
+            for j in range(J):
+                nc.tensor.transpose(tlp[:, j, :], t_src[a][:, j * R:(j + 1) * R], ident_b[:])
+            tT[a] = ttp.tile([P, J, P], BF16, name="tT")
+            nc.vector.tensor_copy(out=tT[a][:], in_=tlp[:])
+
+        def lora_b_transposes():
+            lbp = psum.tile([P, 8, P], BF16, name="lbp", tag="acc", bufs=2)
+            for l in range(8):
+                nc.tensor.transpose(lbp[:, l, :], lb_sb[:, l * R:(l + 1) * R], ident_b[:])
+            nc.vector.tensor_copy(out=lbT[:].rearrange("p a (h l) -> p a h l", l=8),
+                                  in_=lbp[:].rearrange("p l (a h) -> p a h l", a=A))
+
+        def lora_matmuls(a):
+            for h in range(2):
+                dl = psum.tile([P, 4 * O], F32, name="dl", tag="xt", bufs=6)
+                for j in range(4):
+                    nc.tensor.matmul(dl[:, j * O:(j + 1) * O], lhsT=tT[a][:, h * 4 + j, :],
+                                     rhs=lbT[:, a, :], start=True, stop=True)
+                dst = o_sb[a][:, h * 4 * O:(h + 1) * 4 * O]
+                if h == 1 and a % 2 == 0:
+                    nc.vector.tensor_scalar_mul(out=dst, in0=dl[:], scalar1=2.0)
+                else:
+                    nc.scalar.mul(out=dst, in_=dl[:], mul=2.0)
+
+        def warm_up(n):
+            wps = psum.tile([P, 512], F32, name="wps", tag="xt", bufs=6)
+            for i in range(n):
+                nc.tensor.matmul(wps[:], lhsT=warm[:, 0:P], rhs=warm[:], start=True, stop=True)
+
+        warm_up(5)
+        lora_transposes(0)
+        warm_up(1)
+        lora_b_transposes()
+        warm_up(1)
+        for a in range(1, A + 1):
+            if a < A:
+                lora_transposes(a)
+            if a == 2:
+                wp = psum.tile([P, 4, P], F32, name="wp", tag="xt", bufs=6)
+                for u in range(4):
+                    nc.tensor.transpose(wp[:, u, :], w_sb[:].bitcast(F32)[:, words_of(u)], ident_f[:])
+                words_out(False, w_grp[:].bitcast(F32), wp)
+            if a == 4:
+                nc.vector.quantize_mx(out=w_codes[:].bitcast(FP8X4), scales=w_scales[:], in_=w_grp[:])
+            if a - 1 != LATE_ADAPTER:
+                lora_matmuls(a - 1)
+
+        grp = {}
+        codes = {}
+        scales = {}
+        late = {}
+
+        def transposes(u):
+            grp[u] = gpool.tile([P, 4, K], BF16, name="grp", align_bytes=64)
+            late[u] = []
+            for i, t in enumerate(UNITS[u]):
+                xt = psum.tile([P, 4, P], F32, name="xt", tag="xt", bufs=6)
+                for q in range(4):
+                    nc.tensor.transpose(xt[:, q, :], x_words[t][:, words_of(q)], ident_f[:])
+                if t in V_BANKS:
+                    late[u].append((i, xt))
+                else:
+                    words_out(False, grp[u][:].bitcast(F32)[:, i, :], xt)
+
+        def vector_copies(u):
+            for (i, xt) in late[u]:
+                words_out(True, grp[u][:].bitcast(F32)[:, i, :], xt)
+
+        def quantise(u):
+            n = len(UNITS[u])
+            codes[u] = cpool.tile([P, K], U32, name="codes", align_bytes=64)
+            scales[u] = cpool.tile([P, K], U8, name="scales", align_bytes=64)
+            nc.vector.quantize_mx(out=codes[u][:, 0:n * K // 4].bitcast(FP8X4), scales=scales[u][:, 0:n * K // 4],
+                                  in_=grp[u][:, 0:n, :].rearrange("p j k -> p (j k)"))
+
+        def multiply_add_store(u):
+            n = len(UNITS[u])
+            acc = psum.tile([P, 4 * O], F32, name="acc", tag="acc", bufs=2)
+            for i in range(n):
+                for g in range(2):
+                    c0 = (i * 2 + g) * P
+                    nc.tensor.matmul_mx(
+                        out=acc[:, i * O:(i + 1) * O],
+                        lhsT=codes[u][:, c0:c0 + P].bitcast(FP8X4),
+                        lhsT_scale=scales[u][:, c0:c0 + P],
+                        rhs=w_codes[:, g * O:(g + 1) * O].bitcast(FP8X4),
+                        rhs_scale=w_scales[:, g * O:(g + 1) * O],
+                        start=(g == 0), stop=(g == 1))
+            a, j0 = divmod(UNITS[u][0], J)
+            dst = o_sb[a][:, j0 * O:(j0 + n) * O]
+            nc.vector.tensor_tensor(out=dst, in0=acc[:, 0:n * O], in1=dst, op=ADD)
+            if u in STORES:
+                first = UNITS[STORES[u][0]][0] % J
+                last = UNITS[STORES[u][-1]][-1] % J
+                nc.sync.dma_start(out=out_v[a][:, first * O:(last + 1) * O], in_=o_sb[a][:, first * O:(last + 1) * O])
+
+        n_groups = len(GROUPS)
+        for i in range(n_groups + 2):
+            for u in (GROUPS[i] if i < n_groups else []):
+                transposes(u)
+            if i == n_groups - 1:
+                lora_matmuls(LATE_ADAPTER)
+            for u in (GROUPS[i - 1] if 0 <= i - 1 < n_groups else []):
+                quantise(u)
+            for u in (GROUPS[i] if i < n_groups else []):
+                vector_copies(u)
+            for u in (GROUPS[i - 2] if 0 <= i - 2 < n_groups else []):
+                multiply_add_store(u)

@@ -24,6 +24,7 @@ GROUPS = [[u] for u in range(16)]
 STORES = dict([(u, [u]) for u in range(16)])
 LATE_ADAPTER = 7
 V_BANKS = frozenset(range(3, 64, 8))
+N_PERM = 2
 
 
 def words_of(q):
@@ -40,6 +41,7 @@ def tile_linear_pa_t_kernel(tc, data, W, t_lora, lora_b, out):
         ttp = ctx.enter_context(tc.tile_pool(name="ttp", bufs=3))
         gpool = ctx.enter_context(tc.tile_pool(name="gpool", bufs=4))
         cpool = ctx.enter_context(tc.tile_pool(name="cpool", bufs=4))
+        ppool = ctx.enter_context(tc.tile_pool(name="ppool", bufs=3))
         psum = ctx.enter_context(tc.psum_pool(name="psum", bufs=1))
 
         data_v = data.rearrange("a (p j) k -> a p j k", j=J)
@@ -70,11 +72,13 @@ def tile_linear_pa_t_kernel(tc, data, W, t_lora, lora_b, out):
         nc.sync.dma_start(out=w_sb[:], in_=W)
         load_t(2, 2)
         load_t(4, 4)
+        x_units = []
         x_words = {}
         for c in range(2 * A):
             a, h = divmod(c, 2)
             x_half = xpool.tile([P, J // 2, K], BF16, name="x_half", bufs=10)
             nc.sync.dma_start(out=x_half[:], in_=data_v[a, :, h * 4:(h + 1) * 4, :])
+            x_units.append(x_half)
             for j in range(4):
                 x_words[c * 4 + j] = x_half[:].bitcast(F32)[:, j, :]
 
@@ -125,6 +129,14 @@ def tile_linear_pa_t_kernel(tc, data, W, t_lora, lora_b, out):
             for i in range(n):
                 nc.tensor.matmul(wps[:], lhsT=warm[:, 0:P], rhs=warm[:], start=True, stop=True)
 
+        ordered = {}
+
+        def put_in_order(u):
+            ordered[u] = ppool.tile([P, N_PERM, K // 2], F32, name="ordered")
+            nc.vector.tensor_copy(
+                out=ordered[u][:].rearrange("p j (g u m) -> p (j g) u m", g=2, u=2),
+                in_=x_units[u][:].bitcast(F32)[:, 0:N_PERM, :].rearrange("p j (g m u) -> p (j g) u m", g=2, u=2))
+
         warm_up(5)
         lora_transposes(0)
         warm_up(1)
@@ -140,6 +152,10 @@ def tile_linear_pa_t_kernel(tc, data, W, t_lora, lora_b, out):
                 words_out(False, w_grp[:].bitcast(F32), wp)
             if a == 4:
                 nc.vector.quantize_mx(out=w_codes[:].bitcast(FP8X4), scales=w_scales[:], in_=w_grp[:])
+            if a == 6:
+                put_in_order(0)
+            if a == 8:
+                put_in_order(1)
             if a - 1 != LATE_ADAPTER:
                 lora_matmuls(a - 1)
 
@@ -154,7 +170,11 @@ def tile_linear_pa_t_kernel(tc, data, W, t_lora, lora_b, out):
             for i, t in enumerate(UNITS[u]):
                 xt = psum.tile([P, 4, P], F32, name="xt", tag="xt", bufs=6)
                 for q in range(4):
-                    nc.tensor.transpose(xt[:, q, :], x_words[t][:, words_of(q)], ident_f[:])
+                    if i < N_PERM:
+                        words = ordered[u][:, i, q * P:(q + 1) * P]
+                    else:
+                        words = x_words[t][:, words_of(q)]
+                    nc.tensor.transpose(xt[:, q, :], words, ident_f[:])
                 if t in V_BANKS:
                     late[u].append((i, xt))
                 else:
@@ -198,6 +218,8 @@ def tile_linear_pa_t_kernel(tc, data, W, t_lora, lora_b, out):
                 transposes(u)
             if i == n_groups - 1:
                 lora_matmuls(LATE_ADAPTER)
+            if 2 <= i + 1 < n_groups:
+                put_in_order(i + 1)
             for u in (GROUPS[i - 1] if 0 <= i - 1 < n_groups else []):
                 quantise(u)
             for u in (GROUPS[i] if i < n_groups else []):

@@ -5,6 +5,7 @@ from concourse.masks import make_identity
 
 F32 = mybir.dt.float32
 BF16 = mybir.dt.bfloat16
+I32 = mybir.dt.int32
 U32 = mybir.dt.uint32
 U8 = mybir.dt.uint8
 FP8X4 = mybir.dt.float8_e4m3fn_x4
@@ -14,20 +15,19 @@ P = 128
 A = 8
 S = 1024
 K = 1024
+WORDS = K // 2
 O = 128
 R = 128
 J = 8
+T = 4
+UNITS = A * J // T
 FLOPS = 2 * A * S * K * O + 2 * A * S * R * O
 
-UNITS = [list(range(4 * c, 4 * c + 4)) for c in range(16)]
-GROUPS = [[u] for u in range(16)]
-STORES = dict([(u, [u]) for u in range(16)])
-LATE_ADAPTER = 7
-V_BANKS = frozenset(range(3, 64, 8))
-N_PERM = 2
+N_STEPPED = 1
+WARM_UP = 8
 
 
-def words_of(q):
+def stepped_words(q):
     g, u = divmod(q, 2)
     return slice(256 * g + u, 256 * (g + 1), 2)
 
@@ -37,11 +37,11 @@ def tile_linear_pa_t_kernel(tc, data, W, t_lora, lora_b, out):
     with ExitStack() as ctx:
         ctx.enter_context(tc.manual_schedule())
         const = ctx.enter_context(tc.tile_pool(name="const", bufs=1))
-        xpool = ctx.enter_context(tc.tile_pool(name="xpool", bufs=5))
-        ttp = ctx.enter_context(tc.tile_pool(name="ttp", bufs=3))
-        gpool = ctx.enter_context(tc.tile_pool(name="gpool", bufs=4))
-        cpool = ctx.enter_context(tc.tile_pool(name="cpool", bufs=4))
-        ppool = ctx.enter_context(tc.tile_pool(name="ppool", bufs=3))
+        xpool = ctx.enter_context(tc.tile_pool(name="xpool", bufs=10))
+        opool = ctx.enter_context(tc.tile_pool(name="opool", bufs=3))
+        gpool = ctx.enter_context(tc.tile_pool(name="gpool", bufs=3))
+        cpool = ctx.enter_context(tc.tile_pool(name="cpool", bufs=3))
+        tpool = ctx.enter_context(tc.tile_pool(name="tpool", bufs=3))
         psum = ctx.enter_context(tc.psum_pool(name="psum", bufs=1))
 
         data_v = data.rearrange("a (p j) k -> a p j k", j=J)
@@ -50,179 +50,154 @@ def tile_linear_pa_t_kernel(tc, data, W, t_lora, lora_b, out):
         lb_v = lora_b.rearrange("a (h l) r -> (a h) (l r)", l=8)
 
         warm = const.tile([P, 512], BF16, name="warm")
-        nc.vector.memset(warm[:].bitcast(mybir.dt.int32), 0)
+        nc.vector.memset(warm[:].bitcast(I32), 0)
         ident_b = const.tile([P, P], BF16, name="ident_b")
         ident_f = const.tile([P, P], F32, name="ident_f")
         make_identity(nc, ident_b[:])
         make_identity(nc, ident_f[:])
 
         t_src = {}
+        x_units = {}
 
-        def load_t(a0, n):
-            t_sb = const.tile([P, n, J * R], BF16, name="t_sb%d" % a0)
-            nc.sync.dma_start(out=t_sb[:], in_=t_v[:, a0:a0 + n, :])
-            for i in range(n):
-                t_src[a0 + i] = t_sb[:, i, :]
+        def load_t(a):
+            t_src[a] = const.tile([P, J * R], BF16, name="t_sb%d" % a)
+            nc.sync.dma_start(out=t_src[a][:], in_=t_v[:, a, :])
 
-        load_t(0, 1)
+        def load_x(u, pieces):
+            a, h = divmod(u, 2)
+            x_units[u] = xpool.tile([P, T, K], BF16, name="x_unit")
+            n = T // pieces
+            for c in range(pieces):
+                nc.sync.dma_start(out=x_units[u][:, c * n:(c + 1) * n, :],
+                                  in_=data_v[a, :, h * T + c * n:h * T + (c + 1) * n, :])
+
+        load_x(0, 2)
+        load_t(0)
         lb_sb = const.tile([P, 8 * R], BF16, name="lb_sb")
         nc.sync.dma_start(out=lb_sb[:], in_=lb_v)
-        load_t(1, 1)
         w_sb = const.tile([P, K], BF16, name="w_sb")
         nc.sync.dma_start(out=w_sb[:], in_=W)
-        load_t(2, 2)
-        load_t(4, 4)
-        x_units = []
-        x_words = {}
-        for c in range(2 * A):
-            a, h = divmod(c, 2)
-            x_half = xpool.tile([P, J // 2, K], BF16, name="x_half", bufs=10)
-            nc.sync.dma_start(out=x_half[:], in_=data_v[a, :, h * 4:(h + 1) * 4, :])
-            x_units.append(x_half)
-            for j in range(4):
-                x_words[c * 4 + j] = x_half[:].bitcast(F32)[:, j, :]
+        for u in range(1, UNITS):
+            load_x(u, 1)
+            if u % 2 == 1 and u + 1 < UNITS:
+                load_t((u + 1) // 2)
 
-        o_sb = [const.tile([P, J * O], F32, name="o_sb%d" % a) for a in range(A)]
-
-        def words_out(on_vector, dst_f32, bank):
-            src = bank[:].rearrange("p (g u) t -> p g t u", u=2)
-            dst = dst_f32.rearrange("p (g t u) -> p g t u", g=2, u=2)
-            if on_vector:
-                nc.vector.tensor_copy(out=dst, in_=src)
-            else:
-                nc.scalar.copy(out=dst, in_=src)
-
+        o_sb = [const.tile([P, T * O], F32, name="o_sb%d" % u) for u in range(UNITS)]
         lbT = const.tile([P, A, O], BF16, name="lbT")
         w_grp = const.tile([P, K], BF16, name="w_grp", align_bytes=64)
         w_codes = const.tile([P, K // 4], U32, name="w_codes", align_bytes=64)
         w_scales = const.tile([P, K // 4], U8, name="w_scales", align_bytes=64)
         tT = {}
 
-        def lora_transposes(a):
-            tlp = psum.tile([P, J, P], BF16, name="tlp", tag="acc", bufs=2)
-            for j in range(J):
-                nc.tensor.transpose(tlp[:, j, :], t_src[a][:, j * R:(j + 1) * R], ident_b[:])
-            tT[a] = ttp.tile([P, J, P], BF16, name="tT")
-            nc.vector.tensor_copy(out=tT[a][:], in_=tlp[:])
+        def bank(shape, dtype):
+            b = psum.tile(shape, dtype, name="xt", tag="xt", bufs=6)
+            return b
+
+        def words_out(dst_f32, src_bank):
+            nc.scalar.copy(out=dst_f32.rearrange("p (g t u) -> p g t u", g=2, u=2),
+                           in_=src_bank[:].rearrange("p (g u) t -> p g t u", u=2))
+
+        def lora_transposes(u):
+            a, h = divmod(u, 2)
+            tp = bank([P, T, P], BF16)
+            for i in range(T):
+                j = h * T + i
+                nc.tensor.transpose(tp[:, i, :], t_src[a][:, j * R:(j + 1) * R], ident_b[:])
+            tT[u] = tpool.tile([P, T, P], BF16, name="tT")
+            nc.vector.tensor_copy(out=tT[u][:], in_=tp[:])
 
         def lora_b_transposes():
-            lbp = psum.tile([P, 8, P], BF16, name="lbp", tag="acc", bufs=2)
+            lp = bank([P, 8, P], BF16)
             for l in range(8):
-                nc.tensor.transpose(lbp[:, l, :], lb_sb[:, l * R:(l + 1) * R], ident_b[:])
+                nc.tensor.transpose(lp[:, l, :], lb_sb[:, l * R:(l + 1) * R], ident_b[:])
             nc.vector.tensor_copy(out=lbT[:].rearrange("p a (h l) -> p a h l", l=8),
-                                  in_=lbp[:].rearrange("p l (a h) -> p a h l", a=A))
+                                  in_=lp[:].rearrange("p l (a h) -> p a h l", a=A))
 
-        def lora_matmuls(a):
-            for h in range(2):
-                dl = psum.tile([P, 4 * O], F32, name="dl", tag="xt", bufs=6)
-                for j in range(4):
-                    nc.tensor.matmul(dl[:, j * O:(j + 1) * O], lhsT=tT[a][:, h * 4 + j, :],
-                                     rhs=lbT[:, a, :], start=True, stop=True)
-                dst = o_sb[a][:, h * 4 * O:(h + 1) * 4 * O]
-                if h == 1 and a % 2 == 0:
-                    nc.vector.tensor_scalar_mul(out=dst, in0=dl[:], scalar1=2.0)
-                else:
-                    nc.scalar.mul(out=dst, in_=dl[:], mul=2.0)
+        def lora_product(u):
+            dl = bank([P, T * O], F32)
+            for i in range(T):
+                nc.tensor.matmul(dl[:, i * O:(i + 1) * O], lhsT=tT[u][:, i, :],
+                                 rhs=lbT[:, u // 2, :], start=True, stop=True)
+            nc.scalar.mul(out=o_sb[u][:], in_=dl[:], mul=2.0)
 
-        def warm_up(n):
-            wps = psum.tile([P, 512], F32, name="wps", tag="xt", bufs=6)
-            for i in range(n):
-                nc.tensor.matmul(wps[:], lhsT=warm[:, 0:P], rhs=warm[:], start=True, stop=True)
+        def w_transposes():
+            wp = bank([P, 4, P], F32)
+            for q in range(4):
+                nc.tensor.transpose(wp[:, q, :], w_sb[:].bitcast(F32)[:, stepped_words(q)], ident_f[:])
+            words_out(w_grp[:].bitcast(F32), wp)
 
         ordered = {}
 
         def put_in_order(u):
-            ordered[u] = ppool.tile([P, N_PERM, K // 2], F32, name="ordered")
+            n = T - N_STEPPED
+            ordered[u] = opool.tile([P, n, WORDS], F32, name="ordered")
             nc.vector.tensor_copy(
                 out=ordered[u][:].rearrange("p j (g u m) -> p (j g) u m", g=2, u=2),
-                in_=x_units[u][:].bitcast(F32)[:, 0:N_PERM, :].rearrange("p j (g m u) -> p (j g) u m", g=2, u=2))
-
-        warm_up(5)
-        lora_transposes(0)
-        warm_up(1)
-        lora_b_transposes()
-        warm_up(1)
-        for a in range(1, A + 1):
-            if a < A:
-                lora_transposes(a)
-            if a == 2:
-                wp = psum.tile([P, 4, P], F32, name="wp", tag="xt", bufs=6)
-                for u in range(4):
-                    nc.tensor.transpose(wp[:, u, :], w_sb[:].bitcast(F32)[:, words_of(u)], ident_f[:])
-                words_out(False, w_grp[:].bitcast(F32), wp)
-            if a == 4:
-                nc.vector.quantize_mx(out=w_codes[:].bitcast(FP8X4), scales=w_scales[:], in_=w_grp[:])
-            if a == 6:
-                put_in_order(0)
-            if a == 8:
-                put_in_order(1)
-            if a - 1 != LATE_ADAPTER:
-                lora_matmuls(a - 1)
+                in_=x_units[u][:].bitcast(F32)[:, N_STEPPED:T, :].rearrange("p j (g m u) -> p (j g) u m", g=2, u=2))
 
         grp = {}
         codes = {}
         scales = {}
-        late = {}
+        acc = {}
 
         def transposes(u):
-            grp[u] = gpool.tile([P, 4, K], BF16, name="grp", align_bytes=64)
-            late[u] = []
-            for i, t in enumerate(UNITS[u]):
-                xt = psum.tile([P, 4, P], F32, name="xt", tag="xt", bufs=6)
+            grp[u] = gpool.tile([P, T, K], BF16, name="grp", align_bytes=64)
+            for i in range(T):
+                xt = bank([P, 4, P], F32)
                 for q in range(4):
-                    if i < N_PERM:
-                        words = ordered[u][:, i, q * P:(q + 1) * P]
+                    if i < N_STEPPED:
+                        words = x_units[u][:].bitcast(F32)[:, i, stepped_words(q)]
                     else:
-                        words = x_words[t][:, words_of(q)]
+                        words = ordered[u][:, i - N_STEPPED, q * P:(q + 1) * P]
                     nc.tensor.transpose(xt[:, q, :], words, ident_f[:])
-                if t in V_BANKS:
-                    late[u].append((i, xt))
-                else:
-                    words_out(False, grp[u][:].bitcast(F32)[:, i, :], xt)
-
-        def vector_copies(u):
-            for (i, xt) in late[u]:
-                words_out(True, grp[u][:].bitcast(F32)[:, i, :], xt)
+                words_out(grp[u][:].bitcast(F32)[:, i, :], xt)
 
         def quantise(u):
-            n = len(UNITS[u])
-            codes[u] = cpool.tile([P, K], U32, name="codes", align_bytes=64)
-            scales[u] = cpool.tile([P, K], U8, name="scales", align_bytes=64)
-            nc.vector.quantize_mx(out=codes[u][:, 0:n * K // 4].bitcast(FP8X4), scales=scales[u][:, 0:n * K // 4],
-                                  in_=grp[u][:, 0:n, :].rearrange("p j k -> p (j k)"))
+            codes[u] = cpool.tile([P, T * K // 4], U32, name="codes", align_bytes=64)
+            scales[u] = cpool.tile([P, T * K // 4], U8, name="scales", align_bytes=64)
+            nc.vector.quantize_mx(out=codes[u][:].bitcast(FP8X4), scales=scales[u][:],
+                                  in_=grp[u][:].rearrange("p j k -> p (j k)"))
 
-        def multiply_add_store(u):
-            n = len(UNITS[u])
-            acc = psum.tile([P, 4 * O], F32, name="acc", tag="acc", bufs=2)
-            for i in range(n):
+        def multiply(u):
+            acc[u] = psum.tile([P, T * O], F32, name="acc", tag="acc", bufs=2)
+            for i in range(T):
                 for g in range(2):
                     c0 = (i * 2 + g) * P
                     nc.tensor.matmul_mx(
-                        out=acc[:, i * O:(i + 1) * O],
+                        out=acc[u][:, i * O:(i + 1) * O],
                         lhsT=codes[u][:, c0:c0 + P].bitcast(FP8X4),
                         lhsT_scale=scales[u][:, c0:c0 + P],
                         rhs=w_codes[:, g * O:(g + 1) * O].bitcast(FP8X4),
                         rhs_scale=w_scales[:, g * O:(g + 1) * O],
                         start=(g == 0), stop=(g == 1))
-            a, j0 = divmod(UNITS[u][0], J)
-            dst = o_sb[a][:, j0 * O:(j0 + n) * O]
-            nc.vector.tensor_tensor(out=dst, in0=acc[:, 0:n * O], in1=dst, op=ADD)
-            if u in STORES:
-                first = UNITS[STORES[u][0]][0] % J
-                last = UNITS[STORES[u][-1]][-1] % J
-                nc.sync.dma_start(out=out_v[a][:, first * O:(last + 1) * O], in_=o_sb[a][:, first * O:(last + 1) * O])
 
-        n_groups = len(GROUPS)
-        for i in range(n_groups + 2):
-            for u in (GROUPS[i] if i < n_groups else []):
-                transposes(u)
-            if i == n_groups - 1:
-                lora_matmuls(LATE_ADAPTER)
-            if 2 <= i + 1 < n_groups:
+        def add_store(u):
+            nc.vector.tensor_tensor(out=o_sb[u][:], in0=acc[u][:], in1=o_sb[u][:], op=ADD)
+            a, h = divmod(u, 2)
+            nc.sync.dma_start(out=out_v[a][:, h * T * O:(h + 1) * T * O], in_=o_sb[u][:])
+
+        wps = bank([P, 512], F32)
+        for i in range(WARM_UP):
+            nc.tensor.matmul(wps[:], lhsT=warm[:, 0:P], rhs=warm[:], start=True, stop=True)
+        put_in_order(0)
+        for i in range(UNITS + 3):
+            if i < UNITS:
+                transposes(i)
+            if i == 0:
+                lora_transposes(0)
+                lora_b_transposes()
+                w_transposes()
+            if i == 1:
+                nc.vector.quantize_mx(out=w_codes[:].bitcast(FP8X4), scales=w_scales[:], in_=w_grp[:])
+            if i + 1 < UNITS:
                 put_in_order(i + 1)
-            for u in (GROUPS[i - 1] if 0 <= i - 1 < n_groups else []):
-                quantise(u)
-            for u in (GROUPS[i] if i < n_groups else []):
-                vector_copies(u)
-            for u in (GROUPS[i - 2] if 0 <= i - 2 < n_groups else []):
-                multiply_add_store(u)
+            if 0 <= i - 1 < UNITS:
+                quantise(i - 1)
+            if i + 1 < UNITS:
+                lora_transposes(i + 1)
+            if i < UNITS:
+                lora_product(i)
+            if 0 <= i - 3 < UNITS:
+                add_store(i - 3)
+            if 0 <= i - 2 < UNITS:
+                multiply(i - 2)

@@ -132,8 +132,8 @@ def tile_linear_pa_t_kernel(tc, data, W, t_lora, lora_b, out):
             n = T - N_STEPPED
             ordered[u] = opool.tile([P, n, WORDS], F32, name="ordered")
             nc.vector.tensor_copy(
-                out=ordered[u][:].rearrange("p j (g u m) -> p (j g) u m", g=2, u=2),
-                in_=x_units[u][:].bitcast(F32)[:, N_STEPPED:T, :].rearrange("p j (g m u) -> p (j g) u m", g=2, u=2))
+                out=ordered[u][:].rearrange("p j (g u m) -> p (j g) m u", g=2, u=2),
+                in_=x_units[u][:].bitcast(F32)[:, N_STEPPED:T, :].rearrange("p j (g m u) -> p (j g) m u", g=2, u=2))
 
         grp = {}
         codes = {}

@@ -24,7 +24,7 @@ UNITS = A * J // T
 FLOPS = 2 * A * S * K * O + 2 * A * S * R * O
 
 N_STEPPED = 1
-WARM_UP = 8
+WARM_UP = 5
 
 
 def stepped_words(q):
@@ -38,10 +38,10 @@ def tile_linear_pa_t_kernel(tc, data, W, t_lora, lora_b, out):
         ctx.enter_context(tc.manual_schedule())
         const = ctx.enter_context(tc.tile_pool(name="const", bufs=1))
         xpool = ctx.enter_context(tc.tile_pool(name="xpool", bufs=10))
-        opool = ctx.enter_context(tc.tile_pool(name="opool", bufs=3))
+        opool = ctx.enter_context(tc.tile_pool(name="opool", bufs=4))
         gpool = ctx.enter_context(tc.tile_pool(name="gpool", bufs=3))
         cpool = ctx.enter_context(tc.tile_pool(name="cpool", bufs=3))
-        tpool = ctx.enter_context(tc.tile_pool(name="tpool", bufs=3))
+        tpool = ctx.enter_context(tc.tile_pool(name="tpool", bufs=4))
         psum = ctx.enter_context(tc.psum_pool(name="psum", bufs=1))
 
         data_v = data.rearrange("a (p j) k -> a p j k", j=J)
@@ -63,24 +63,21 @@ def tile_linear_pa_t_kernel(tc, data, W, t_lora, lora_b, out):
             t_src[a] = const.tile([P, J * R], BF16, name="t_sb%d" % a)
             nc.sync.dma_start(out=t_src[a][:], in_=t_v[:, a, :])
 
-        def load_x(u, pieces):
+        def load_x(u):
             a, h = divmod(u, 2)
             x_units[u] = xpool.tile([P, T, K], BF16, name="x_unit")
-            n = T // pieces
-            for c in range(pieces):
-                nc.sync.dma_start(out=x_units[u][:, c * n:(c + 1) * n, :],
-                                  in_=data_v[a, :, h * T + c * n:h * T + (c + 1) * n, :])
+            nc.sync.dma_start(out=x_units[u][:], in_=data_v[a, :, h * T:(h + 1) * T, :])
 
-        load_x(0, 2)
         load_t(0)
         lb_sb = const.tile([P, 8 * R], BF16, name="lb_sb")
         nc.sync.dma_start(out=lb_sb[:], in_=lb_v)
+        for a in range(1, A):
+            load_t(a)
+        load_x(0)
         w_sb = const.tile([P, K], BF16, name="w_sb")
         nc.sync.dma_start(out=w_sb[:], in_=W)
         for u in range(1, UNITS):
-            load_x(u, 1)
-            if u % 2 == 1 and u + 1 < UNITS:
-                load_t((u + 1) // 2)
+            load_x(u)
 
         o_sb = [const.tile([P, T * O], F32, name="o_sb%d" % u) for u in range(UNITS)]
         lbT = const.tile([P, A, O], BF16, name="lbT")
@@ -97,14 +94,15 @@ def tile_linear_pa_t_kernel(tc, data, W, t_lora, lora_b, out):
             nc.scalar.copy(out=dst_f32.rearrange("p (g t u) -> p g t u", g=2, u=2),
                            in_=src_bank[:].rearrange("p (g u) t -> p g t u", u=2))
 
-        def lora_transposes(u):
-            a, h = divmod(u, 2)
-            tp = bank([P, T, P], BF16)
-            for i in range(T):
-                j = h * T + i
-                nc.tensor.transpose(tp[:, i, :], t_src[a][:, j * R:(j + 1) * R], ident_b[:])
-            tT[u] = tpool.tile([P, T, P], BF16, name="tT")
-            nc.vector.tensor_copy(out=tT[u][:], in_=tp[:])
+        def lora_transposes(a):
+            tp = bank([P, J, P], BF16)
+            for j in range(J):
+                nc.tensor.transpose(tp[:, j, :], t_src[a][:, j * R:(j + 1) * R], ident_b[:])
+            tT[a] = tpool.tile([P, J, P], BF16, name="tT")
+            if a % 2 == 0:
+                nc.vector.tensor_copy(out=tT[a][:], in_=tp[:])
+            else:
+                nc.scalar.copy(out=tT[a][:], in_=tp[:])
 
         def lora_b_transposes():
             lp = bank([P, 8, P], BF16)
@@ -113,12 +111,16 @@ def tile_linear_pa_t_kernel(tc, data, W, t_lora, lora_b, out):
             nc.vector.tensor_copy(out=lbT[:].rearrange("p a (h l) -> p a h l", l=8),
                                   in_=lp[:].rearrange("p l (a h) -> p a h l", a=A))
 
-        def lora_product(u):
-            dl = bank([P, T * O], F32)
-            for i in range(T):
-                nc.tensor.matmul(dl[:, i * O:(i + 1) * O], lhsT=tT[u][:, i, :],
-                                 rhs=lbT[:, u // 2, :], start=True, stop=True)
-            nc.scalar.mul(out=o_sb[u][:], in_=dl[:], mul=2.0)
+        def lora_product(a):
+            for h in range(2):
+                dl = bank([P, T * O], F32)
+                for i in range(T):
+                    nc.tensor.matmul(dl[:, i * O:(i + 1) * O], lhsT=tT[a][:, h * T + i, :],
+                                     rhs=lbT[:, a, :], start=True, stop=True)
+                if a % 2 == 0 and h == 0:
+                    nc.vector.tensor_scalar_mul(out=o_sb[2 * a + h][:], in0=dl[:], scalar1=2.0)
+                else:
+                    nc.scalar.mul(out=o_sb[2 * a + h][:], in_=dl[:], mul=2.0)
 
         def w_transposes():
             wp = bank([P, 4, P], F32)
@@ -179,24 +181,30 @@ def tile_linear_pa_t_kernel(tc, data, W, t_lora, lora_b, out):
         wps = bank([P, 512], F32)
         for i in range(WARM_UP):
             nc.tensor.matmul(wps[:], lhsT=warm[:, 0:P], rhs=warm[:], start=True, stop=True)
-        put_in_order(0)
+        lora_transposes(0)
+        lora_b_transposes()
+        lora_transposes(1)
+        for a in range(2, A + 2, 2):
+            if a < A:
+                lora_transposes(a)
+                lora_transposes(a + 1)
+            if a == A:
+                w_transposes()
+            lora_product(a - 2)
+            lora_product(a - 1)
+            if a == 6:
+                put_in_order(0)
+        put_in_order(1)
+
         for i in range(UNITS + 3):
             if i < UNITS:
                 transposes(i)
             if i == 0:
-                lora_transposes(0)
-                lora_b_transposes()
-                w_transposes()
-            if i == 1:
                 nc.vector.quantize_mx(out=w_codes[:].bitcast(FP8X4), scales=w_scales[:], in_=w_grp[:])
-            if i + 1 < UNITS:
-                put_in_order(i + 1)
             if 0 <= i - 1 < UNITS:
                 quantise(i - 1)
-            if i + 1 < UNITS:
-                lora_transposes(i + 1)
-            if i < UNITS:
-                lora_product(i)
+            if i + 2 < UNITS:
+                put_in_order(i + 2)
             if 0 <= i - 3 < UNITS:
                 add_store(i - 3)
             if 0 <= i - 2 < UNITS:

@@ -23,7 +23,7 @@ T = 4
 UNITS = A * J // T
 FLOPS = 2 * A * S * K * O + 2 * A * S * R * O
 
-N_STEPPED = 1
+N_STEPPED = 2
 WARM_UP = 5
 
 

@@ -23,7 +23,12 @@ T = 4
 UNITS = A * J // T
 FLOPS = 2 * A * S * K * O + 2 * A * S * R * O
 
-N_STEPPED = 2
+LATE = 7
+
+
+def stepped(u):
+    return 0 if u < 2 else 2
+
 WARM_UP = 5
 
 
@@ -117,7 +122,7 @@ def tile_linear_pa_t_kernel(tc, data, W, t_lora, lora_b, out):
                 for i in range(T):
                     nc.tensor.matmul(dl[:, i * O:(i + 1) * O], lhsT=tT[a][:, h * T + i, :],
                                      rhs=lbT[:, a, :], start=True, stop=True)
-                if a % 2 == 0 and h == 0:
+                if h == 0 and a < 6:
                     nc.vector.tensor_scalar_mul(out=o_sb[2 * a + h][:], in0=dl[:], scalar1=2.0)
                 else:
                     nc.scalar.mul(out=o_sb[2 * a + h][:], in_=dl[:], mul=2.0)
@@ -131,11 +136,11 @@ def tile_linear_pa_t_kernel(tc, data, W, t_lora, lora_b, out):
         ordered = {}
 
         def put_in_order(u):
-            n = T - N_STEPPED
+            n = T - stepped(u)
             ordered[u] = opool.tile([P, n, WORDS], F32, name="ordered")
             nc.vector.tensor_copy(
                 out=ordered[u][:].rearrange("p j (g u m) -> p (j g) m u", g=2, u=2),
-                in_=x_units[u][:].bitcast(F32)[:, N_STEPPED:T, :].rearrange("p j (g m u) -> p (j g) m u", g=2, u=2))
+                in_=x_units[u][:].bitcast(F32)[:, stepped(u):T, :].rearrange("p j (g m u) -> p (j g) m u", g=2, u=2))
 
         grp = {}
         codes = {}
@@ -147,22 +152,25 @@ def tile_linear_pa_t_kernel(tc, data, W, t_lora, lora_b, out):
             for i in range(T):
                 xt = bank([P, 4, P], F32)
                 for q in range(4):
-                    if i < N_STEPPED:
+                    if i < stepped(u):
                         words = x_units[u][:].bitcast(F32)[:, i, stepped_words(q)]
                     else:
-                        words = ordered[u][:, i - N_STEPPED, q * P:(q + 1) * P]
+                        words = ordered[u][:, i - stepped(u), q * P:(q + 1) * P]
                     nc.tensor.transpose(xt[:, q, :], words, ident_f[:])
                 words_out(grp[u][:].bitcast(F32)[:, i, :], xt)
 
-        def quantise(u):
-            codes[u] = cpool.tile([P, T * K // 4], U32, name="codes", align_bytes=64)
-            scales[u] = cpool.tile([P, T * K // 4], U8, name="scales", align_bytes=64)
-            nc.vector.quantize_mx(out=codes[u][:].bitcast(FP8X4), scales=scales[u][:],
-                                  in_=grp[u][:].rearrange("p j k -> p (j k)"))
+        def quantise(u, lo, hi):
+            if lo == 0:
+                codes[u] = cpool.tile([P, T * K // 4], U32, name="codes", align_bytes=64)
+                scales[u] = cpool.tile([P, T * K // 4], U8, name="scales", align_bytes=64)
+            w = slice(lo * K // 4, hi * K // 4)
+            nc.vector.quantize_mx(out=codes[u][:, w].bitcast(FP8X4), scales=scales[u][:, w],
+                                  in_=grp[u][:, lo:hi, :].rearrange("p j k -> p (j k)"))
 
-        def multiply(u):
-            acc[u] = psum.tile([P, T * O], F32, name="acc", tag="acc", bufs=2)
-            for i in range(T):
+        def multiply(u, lo, hi):
+            if lo == 0:
+                acc[u] = psum.tile([P, T * O], F32, name="acc", tag="acc", bufs=2)
+            for i in range(lo, hi):
                 for g in range(2):
                     c0 = (i * 2 + g) * P
                     nc.tensor.matmul_mx(
@@ -173,10 +181,14 @@ def tile_linear_pa_t_kernel(tc, data, W, t_lora, lora_b, out):
                         rhs_scale=w_scales[:, g * O:(g + 1) * O],
                         start=(g == 0), stop=(g == 1))
 
-        def add_store(u):
-            nc.vector.tensor_tensor(out=o_sb[u][:], in0=acc[u][:], in1=o_sb[u][:], op=ADD)
+        def add_store(u, lo, hi):
+            w = slice(lo * O, hi * O)
+            nc.vector.tensor_tensor(out=o_sb[u][:, w], in0=acc[u][:, w], in1=o_sb[u][:, w], op=ADD)
             a, h = divmod(u, 2)
-            nc.sync.dma_start(out=out_v[a][:, h * T * O:(h + 1) * T * O], in_=o_sb[u][:])
+            nc.sync.dma_start(out=out_v[a][:, (h * T + lo) * O:(h * T + hi) * O], in_=o_sb[u][:, w])
+
+        def pieces(u):
+            return [(0, 2), (2, 4)] if u == UNITS - 1 else [(0, T)]
 
         wps = bank([P, 512], F32)
         for i in range(WARM_UP):
@@ -191,7 +203,8 @@ def tile_linear_pa_t_kernel(tc, data, W, t_lora, lora_b, out):
             if a == A:
                 w_transposes()
             lora_product(a - 2)
-            lora_product(a - 1)
+            if a - 1 != LATE:
+                lora_product(a - 1)
             if a == 6:
                 put_in_order(0)
         put_in_order(1)
@@ -199,13 +212,20 @@ def tile_linear_pa_t_kernel(tc, data, W, t_lora, lora_b, out):
         for i in range(UNITS + 3):
             if i < UNITS:
                 transposes(i)
+            if i == UNITS - 1:
+                lora_product(LATE)
             if i == 0:
                 nc.vector.quantize_mx(out=w_codes[:].bitcast(FP8X4), scales=w_scales[:], in_=w_grp[:])
+            if 0 <= i - 3 < UNITS - 1:
+                add_store(i - 3, 0, T)
             if 0 <= i - 1 < UNITS:
-                quantise(i - 1)
+                for lo, hi in pieces(i - 1):
+                    quantise(i - 1, lo, hi)
             if i + 2 < UNITS:
                 put_in_order(i + 2)
-            if 0 <= i - 3 < UNITS:
-                add_store(i - 3)
             if 0 <= i - 2 < UNITS:
-                multiply(i - 2)
+                for lo, hi in pieces(i - 2):
+                    multiply(i - 2, lo, hi)
+            if i == UNITS + 2:
+                for lo, hi in pieces(i - 3):
+                    add_store(i - 3, lo, hi)

@@ -95,9 +95,9 @@ def tile_linear_pa_t_kernel(tc, data, W, t_lora, lora_b, out):
             b = psum.tile(shape, dtype, name="xt", tag="xt", bufs=6)
             return b
 
-        def words_out(dst_f32, src_bank):
-            nc.scalar.copy(out=dst_f32.rearrange("p (g t u) -> p g t u", g=2, u=2),
-                           in_=src_bank[:].rearrange("p (g u) t -> p g t u", u=2))
+        def words_out(dst_f32, src_bank, copy=nc.scalar.copy):
+            copy(out=dst_f32.rearrange("p (g t u) -> p g t u", g=2, u=2),
+                 in_=src_bank[:].rearrange("p (g u) t -> p g t u", u=2))
 
         def lora_transposes(a):
             tp = bank([P, J, P], BF16)
@@ -138,9 +138,10 @@ def tile_linear_pa_t_kernel(tc, data, W, t_lora, lora_b, out):
         def put_in_order(u):
             n = T - stepped(u)
             ordered[u] = opool.tile([P, n, WORDS], F32, name="ordered")
-            nc.vector.tensor_copy(
-                out=ordered[u][:].rearrange("p j (g u m) -> p (j g) m u", g=2, u=2),
-                in_=x_units[u][:].bitcast(F32)[:, stepped(u):T, :].rearrange("p j (g m u) -> p (j g) m u", g=2, u=2))
+            for lo, hi in ([(0, 2), (2, 4)] if u == 0 else [(0, n)]):
+                nc.vector.tensor_copy(
+                    out=ordered[u][:, lo:hi, :].rearrange("p j (g u m) -> p (j g) m u", g=2, u=2),
+                    in_=x_units[u][:].bitcast(F32)[:, stepped(u) + lo:stepped(u) + hi, :].rearrange("p j (g m u) -> p (j g) m u", g=2, u=2))
 
         grp = {}
         codes = {}
@@ -157,7 +158,8 @@ def tile_linear_pa_t_kernel(tc, data, W, t_lora, lora_b, out):
                     else:
                         words = ordered[u][:, i - stepped(u), q * P:(q + 1) * P]
                     nc.tensor.transpose(xt[:, q, :], words, ident_f[:])
-                words_out(grp[u][:].bitcast(F32)[:, i, :], xt)
+                words_out(grp[u][:].bitcast(F32)[:, i, :], xt,
+                          nc.vector.tensor_copy if u == 0 and i % 2 == 1 else nc.scalar.copy)
 
         def quantise(u, lo, hi):
             if lo == 0:
@@ -188,14 +190,21 @@ def tile_linear_pa_t_kernel(tc, data, W, t_lora, lora_b, out):
             nc.sync.dma_start(out=out_v[a][:, (h * T + lo) * O:(h * T + hi) * O], in_=o_sb[u][:, w])
 
         def pieces(u):
-            return [(0, 2), (2, 4)] if u == UNITS - 1 else [(0, T)]
+            return [(0, 2), (2, 3), (3, 4)] if u == UNITS - 1 else [(0, T)]
 
         wps = bank([P, 512], F32)
-        for i in range(WARM_UP):
-            nc.tensor.matmul(wps[:], lhsT=warm[:, 0:P], rhs=warm[:], start=True, stop=True)
+
+        def warm_up(n):
+            for i in range(n):
+                nc.tensor.matmul(wps[:], lhsT=warm[:, 0:P], rhs=warm[:], start=True, stop=True)
+
+        warm_up(WARM_UP)
         lora_transposes(0)
+        warm_up(1)
         lora_b_transposes()
+        warm_up(1)
         lora_transposes(1)
+        warm_up(1)
         for a in range(2, A + 2, 2):
             if a < A:
                 lora_transposes(a)
@@ -216,10 +225,12 @@ def tile_linear_pa_t_kernel(tc, data, W, t_lora, lora_b, out):
                 lora_product(LATE)
             if i == 0:
                 nc.vector.quantize_mx(out=w_codes[:].bitcast(FP8X4), scales=w_scales[:], in_=w_grp[:])
+            if i == UNITS:
+                quantise(i - 1, 0, 2)
             if 0 <= i - 3 < UNITS - 1:
                 add_store(i - 3, 0, T)
             if 0 <= i - 1 < UNITS:
-                for lo, hi in pieces(i - 1):
+                for lo, hi in pieces(i - 1)[(1 if i == UNITS else 0):]:
                     quantise(i - 1, lo, hi)
             if i + 2 < UNITS:
                 put_in_order(i + 2)

from contextlib import ExitStack

import concourse.mybir as mybir
from concourse.masks import make_identity

F32 = mybir.dt.float32
BF16 = mybir.dt.bfloat16
I32 = mybir.dt.int32
U32 = mybir.dt.uint32
U8 = mybir.dt.uint8
FP8X4 = mybir.dt.float8_e4m3fn_x4
ADD = mybir.AluOpType.add

P = 128
A = 8
S = 1024
K = 1024
WORDS = K // 2
O = 128
R = 128
J = 8
T = 4
UNITS = A * J // T
FLOPS = 2 * A * S * K * O + 2 * A * S * R * O

LATE = 7


def stepped(u):
    return 0 if u < 2 else 2

WARM_UP = 5


def stepped_words(q):
    g, u = divmod(q, 2)
    return slice(256 * g + u, 256 * (g + 1), 2)


def tile_linear_pa_t_kernel(tc, data, W, t_lora, lora_b, out):
    nc = tc.nc
    with ExitStack() as ctx:
        ctx.enter_context(tc.manual_schedule())
        const = ctx.enter_context(tc.tile_pool(name="const", bufs=1))
        xpool = ctx.enter_context(tc.tile_pool(name="xpool", bufs=10))
        opool = ctx.enter_context(tc.tile_pool(name="opool", bufs=4))
        gpool = ctx.enter_context(tc.tile_pool(name="gpool", bufs=3))
        cpool = ctx.enter_context(tc.tile_pool(name="cpool", bufs=3))
        tpool = ctx.enter_context(tc.tile_pool(name="tpool", bufs=4))
        psum = ctx.enter_context(tc.psum_pool(name="psum", bufs=1))

        data_v = data.rearrange("a (p j) k -> a p j k", j=J)
        t_v = t_lora.rearrange("a g (p j) r -> p (a g) (j r)", j=J)
        out_v = out.rearrange("a (p j) o -> a p (j o)", j=J)
        lb_v = lora_b.rearrange("a (h l) r -> (a h) (l r)", l=8)

        warm = const.tile([P, 512], BF16, name="warm")
        nc.vector.memset(warm[:].bitcast(I32), 0)
        ident_b = const.tile([P, P], BF16, name="ident_b")
        ident_f = const.tile([P, P], F32, name="ident_f")
        make_identity(nc, ident_b[:])
        make_identity(nc, ident_f[:])

        t_src = {}
        x_units = {}

        def load_t(a):
            t_src[a] = const.tile([P, J * R], BF16, name="t_sb%d" % a)
            nc.sync.dma_start(out=t_src[a][:], in_=t_v[:, a, :])

        def load_x(u):
            a, h = divmod(u, 2)
            x_units[u] = xpool.tile([P, T, K], BF16, name="x_unit")
            nc.sync.dma_start(out=x_units[u][:], in_=data_v[a, :, h * T:(h + 1) * T, :])

        load_t(0)
        lb_sb = const.tile([P, 8 * R], BF16, name="lb_sb")
        nc.sync.dma_start(out=lb_sb[:], in_=lb_v)
        for a in range(1, A):
            load_t(a)
        load_x(0)
        w_sb = const.tile([P, K], BF16, name="w_sb")
        nc.sync.dma_start(out=w_sb[:], in_=W)
        for u in range(1, UNITS):
            load_x(u)

        o_sb = [const.tile([P, T * O], F32, name="o_sb%d" % u) for u in range(UNITS)]
        lbT = const.tile([P, A, O], BF16, name="lbT")
        w_grp = const.tile([P, K], BF16, name="w_grp", align_bytes=64)
        w_codes = const.tile([P, K // 4], U32, name="w_codes", align_bytes=64)
        w_scales = const.tile([P, K // 4], U8, name="w_scales", align_bytes=64)
        tT = {}

        def bank(shape, dtype):
            b = psum.tile(shape, dtype, name="xt", tag="xt", bufs=6)
            return b

        def words_out(dst_f32, src_bank, copy=nc.scalar.copy):
            copy(out=dst_f32.rearrange("p (g t u) -> p g t u", g=2, u=2),
                 in_=src_bank[:].rearrange("p (g u) t -> p g t u", u=2))

        def lora_transposes(a):
            tp = bank([P, J, P], BF16)
            for j in range(J):
                nc.tensor.transpose(tp[:, j, :], t_src[a][:, j * R:(j + 1) * R], ident_b[:])
            tT[a] = tpool.tile([P, J, P], BF16, name="tT")
            if a % 2 == 0:
                nc.vector.tensor_copy(out=tT[a][:], in_=tp[:])
            else:
                nc.scalar.copy(out=tT[a][:], in_=tp[:])

        def lora_b_transposes():
            lp = bank([P, 8, P], BF16)
            for l in range(8):
                nc.tensor.transpose(lp[:, l, :], lb_sb[:, l * R:(l + 1) * R], ident_b[:])
            nc.vector.tensor_copy(out=lbT[:].rearrange("p a (h l) -> p a h l", l=8),
                                  in_=lp[:].rearrange("p l (a h) -> p a h l", a=A))

        def lora_product(a):
            for h in range(2):
                dl = bank([P, T * O], F32)
                for i in range(T):
                    nc.tensor.matmul(dl[:, i * O:(i + 1) * O], lhsT=tT[a][:, h * T + i, :],
                                     rhs=lbT[:, a, :], start=True, stop=True)
                if h == 0 and a < 6:
                    nc.vector.tensor_scalar_mul(out=o_sb[2 * a + h][:], in0=dl[:], scalar1=2.0)
                else:
                    nc.scalar.mul(out=o_sb[2 * a + h][:], in_=dl[:], mul=2.0)

        def w_transposes():
            wp = bank([P, 4, P], F32)
            for q in range(4):
                nc.tensor.transpose(wp[:, q, :], w_sb[:].bitcast(F32)[:, stepped_words(q)], ident_f[:])
            words_out(w_grp[:].bitcast(F32), wp)

        ordered = {}

        def put_in_order(u):
            n = T - stepped(u)
            ordered[u] = opool.tile([P, n, WORDS], F32, name="ordered")
            for lo, hi in ([(0, 2), (2, 4)] if u == 0 else [(0, n)]):
                nc.vector.tensor_copy(
                    out=ordered[u][:, lo:hi, :].rearrange("p j (g u m) -> p (j g) m u", g=2, u=2),
                    in_=x_units[u][:].bitcast(F32)[:, stepped(u) + lo:stepped(u) + hi, :].rearrange("p j (g m u) -> p (j g) m u", g=2, u=2))

        grp = {}
        codes = {}
        scales = {}
        acc = {}

        def transposes(u):
            grp[u] = gpool.tile([P, T, K], BF16, name="grp", align_bytes=64)
            for i in range(T):
                xt = bank([P, 4, P], F32)
                for q in range(4):
                    if i < stepped(u):
                        words = x_units[u][:].bitcast(F32)[:, i, stepped_words(q)]
                    else:
                        words = ordered[u][:, i - stepped(u), q * P:(q + 1) * P]
                    nc.tensor.transpose(xt[:, q, :], words, ident_f[:])
                words_out(grp[u][:].bitcast(F32)[:, i, :], xt,
                          nc.vector.tensor_copy if u == 0 and i % 2 == 1 else nc.scalar.copy)

        def quantise(u, lo, hi):
            if lo == 0:
                codes[u] = cpool.tile([P, T * K // 4], U32, name="codes", align_bytes=64)
                scales[u] = cpool.tile([P, T * K // 4], U8, name="scales", align_bytes=64)
            w = slice(lo * K // 4, hi * K // 4)
            nc.vector.quantize_mx(out=codes[u][:, w].bitcast(FP8X4), scales=scales[u][:, w],
                                  in_=grp[u][:, lo:hi, :].rearrange("p j k -> p (j k)"))

        def multiply(u, lo, hi):
            if lo == 0:
                acc[u] = psum.tile([P, T * O], F32, name="acc", tag="acc", bufs=2)
            for i in range(lo, hi):
                for g in range(2):
                    c0 = (i * 2 + g) * P
                    nc.tensor.matmul_mx(
                        out=acc[u][:, i * O:(i + 1) * O],
                        lhsT=codes[u][:, c0:c0 + P].bitcast(FP8X4),
                        lhsT_scale=scales[u][:, c0:c0 + P],
                        rhs=w_codes[:, g * O:(g + 1) * O].bitcast(FP8X4),
                        rhs_scale=w_scales[:, g * O:(g + 1) * O],
                        start=(g == 0), stop=(g == 1))

        def add_store(u, lo, hi):
            w = slice(lo * O, hi * O)
            nc.vector.tensor_tensor(out=o_sb[u][:, w], in0=acc[u][:, w], in1=o_sb[u][:, w], op=ADD)
            a, h = divmod(u, 2)
            nc.sync.dma_start(out=out_v[a][:, (h * T + lo) * O:(h * T + hi) * O], in_=o_sb[u][:, w])

        def pieces(u):
            return [(0, 2), (2, 3), (3, 4)] if u == UNITS - 1 else [(0, T)]

        wps = bank([P, 512], F32)

        def warm_up(n):
            for i in range(n):
                nc.tensor.matmul(wps[:], lhsT=warm[:, 0:P], rhs=warm[:], start=True, stop=True)

        warm_up(WARM_UP)
        lora_transposes(0)
        warm_up(1)
        lora_b_transposes()
        warm_up(1)
        lora_transposes(1)
        warm_up(1)
        for a in range(2, A + 2, 2):
            if a < A:
                lora_transposes(a)
                lora_transposes(a + 1)
            if a == A:
                w_transposes()
            lora_product(a - 2)
            if a - 1 != LATE:
                lora_product(a - 1)
            if a == 6:
                put_in_order(0)
        put_in_order(1)

        for i in range(UNITS + 3):
            if i < UNITS:
                transposes(i)
            if i == UNITS - 1:
                lora_product(LATE)
            if i == 0:
                nc.vector.quantize_mx(out=w_codes[:].bitcast(FP8X4), scales=w_scales[:], in_=w_grp[:])
            if i == UNITS:
                quantise(i - 1, 0, 2)
            if 0 <= i - 3 < UNITS - 1:
                add_store(i - 3, 0, T)
            if 0 <= i - 1 < UNITS:
                for lo, hi in pieces(i - 1)[(1 if i == UNITS else 0):]:
                    quantise(i - 1, lo, hi)
            if i + 2 < UNITS:
                put_in_order(i + 2)
            if 0 <= i - 2 < UNITS:
                for lo, hi in pieces(i - 2):
                    multiply(i - 2, lo, hi)
            if i == UNITS + 2:
                for lo, hi in pieces(i - 3):
                    add_store(i - 3, lo, hi)
